import numpy as np
import ml_dtypes


def mxq(x, axis, fmt="e4m3"):
    dtype, down = {"e4m3": (ml_dtypes.float8_e4m3fn, 7), "e5m2": (ml_dtypes.float8_e5m2, 14)}[fmt]
    v = np.moveaxis(np.asarray(x, np.float32).astype(ml_dtypes.bfloat16).astype(np.float64), axis, -1)
    blocks = v.reshape(v.shape[:-1] + (-1, 32))
    amax = np.abs(blocks).max(-1, keepdims=True)
    byte = np.maximum(np.where(amax > 0, np.frexp(amax)[1] - 1 + 127, 0) - down, 1)
    scale = np.exp2(byte - 127.0)
    codes = (blocks / scale).astype(np.float32).astype(dtype).astype(np.float64)
    return np.moveaxis((codes * scale).reshape(v.shape), -1, axis)


WIDE = False


def mx_kscale(k):
    if not WIDE:
        return np.ones(k)
    levels = np.array([10, -10, 5, -5, 0])
    a = np.random.permutation(np.resize(levels, k // 512 * 4)).reshape(k // 512, 4)
    idx = np.arange(k)
    return np.exp2(a[idx // 512, idx % 128 // 32])


BF16 = ml_dtypes.bfloat16


def bf(x):
    return np.asarray(x, np.float32).astype(BF16)


def f64(x):
    return np.asarray(x).astype(np.float64)


N, D, T, H, DH = 1, 16384, 128, 2, 512
EPS = 1e-12
A = 6.0
R = 0.2


def l2norm(x):
    n = np.sqrt(np.sum(x * x, axis=-1, keepdims=True))
    return x / np.maximum(n, EPS)


def setup_inputs():
    s = mx_kscale(D)
    return {"rgb": bf(np.random.standard_normal((N, D, T)) * R * s[None, :, None]),
            "rgb_proj": bf(np.random.standard_normal((H, D, DH)) / (R * np.sqrt(D)) / s[None, :, None]),
            "atte_w": bf(np.random.standard_normal((H, DH, DH)) * A)}


def reference(rgb, rgb_proj, atte_w):
    rgb_t = f64(rgb).swapaxes(1, 2)
    p = mxq(rgb_t, 2, "e4m3")[:, None] @ mxq(f64(rgb_proj), 1, "e4m3")[None]
    o_rgb = l2norm(p)
    q_bil = mxq(o_rgb, 3, "e4m3") @ mxq(f64(atte_w), 1, "e4m3")[None]
    return o_rgb, q_bil

@@ -1,0 +1,197 @@
+from contextlib import ExitStack
+
+import concourse.mybir as mybir
+from concourse.masks import make_identity
+
+BF16 = mybir.dt.bfloat16
+F32 = mybir.dt.float32
+U32 = mybir.dt.uint32
+U8 = mybir.dt.uint8
+FP8X4 = mybir.dt.float8_e4m3fn_x4
+ACT = mybir.ActivationFunctionType
+
+P = 128
+PACK = 4
+K_PASS = P * PACK
+
+D, T, H, DH = 16384, 128, 2, 512
+EPS = 1e-12
+
+PROJ_PASSES = 2
+RGB_PASSES = 4
+PROJ_LOADS = D // (PROJ_PASSES * K_PASS)
+PROJ_LOADS_PER_RGB_LOAD = RGB_PASSES // PROJ_PASSES
+RUN = 4
+
+FLOPS = 2 * H * T * D * DH + 2 * H * T * DH * DH
+
+
+def load_and_regroup(nc, raw_pool, grouped_pool, source, passes, width, label):
+    raw = raw_pool.tile([P, passes, PACK, width], BF16, name="raw_" + label, tag="raw_" + label)
+    nc.sync.dma_start(out=raw[:], in_=source)
+    grouped = grouped_pool.tile(
+        [P, passes, width, PACK], BF16, name="grouped_" + label, tag="grouped_" + label, align_bytes=64
+    )
+    for c in range(passes):
+        copy = nc.scalar.copy if c < passes // 2 else nc.vector.tensor_copy
+        copy(
+            out=grouped[:, c, :, :].rearrange("p (g i) j -> p g j i", i=RUN),
+            in_=raw[:, c, :, :].rearrange("p j (g i) -> p g j i", i=RUN),
+        )
+    return grouped
+
+
+def quantise(nc, grouped, codes, scales):
+    nc.vector.quantize_mx(
+        out=codes.bitcast(FP8X4),
+        scales=scales,
+        in_=grouped[:].rearrange("p c w j -> p (c w j)"),
+    )
+
+
+def tile_mca_pa_k_kernel(tc, rgb, rgb_proj, atte_w, out_0, out_1):
+    nc = tc.nc
+    with ExitStack() as ctx:
+        keep = ctx.enter_context(tc.tile_pool(name="keep", bufs=1))
+        raw_pool = ctx.enter_context(tc.tile_pool(name="raw", bufs=8))
+        grouped_pool = ctx.enter_context(tc.tile_pool(name="grouped", bufs=3))
+        mx_pool = ctx.enter_context(tc.tile_pool(name="mx", bufs=3))
+        tail = ctx.enter_context(tc.tile_pool(name="tail", bufs=2))
+        sums = ctx.enter_context(tc.psum_pool(name="sums", bufs=1))
+        psum = ctx.enter_context(tc.psum_pool(name="psum", bufs=2))
+
+        one = keep.tile([P, 1], F32, name="one")
+        nc.vector.memset(one[:], 1.0)
+        root_of_one = keep.tile([P, 1], F32, name="root_of_one")
+        nc.scalar.sqrt(out=root_of_one[:], in_=one[:])
+
+        identity = keep.tile([P, P], BF16, name="identity")
+        make_identity(nc, identity[:])
+
+        rgb_codes = keep.tile([P, D // K_PASS, T], U32, name="rgb_codes", align_bytes=64)
+        rgb_scales = keep.tile([P, D // K_PASS, T], U8, name="rgb_scales", align_bytes=64)
+        atte_codes = keep.tile([P, H, DH], U32, name="atte_codes", align_bytes=64)
+        atte_scales = keep.tile([P, H, DH], U8, name="atte_scales", align_bytes=64)
+
+        p_sum = [sums.tile([T, DH], F32, name="p_sum%d" % h) for h in range(H)]
+
+        def quantise_and_multiply(h, u, grouped):
+            proj_codes = mx_pool.tile([P, PROJ_PASSES, DH], U32, name="proj_codes", align_bytes=64)
+            proj_scales = mx_pool.tile([P, PROJ_PASSES, DH], U8, name="proj_scales", align_bytes=64)
+            quantise(
+                nc,
+                grouped,
+                proj_codes[:].rearrange("p c w -> p (c w)"),
+                proj_scales[:].rearrange("p c w -> p (c w)"),
+            )
+            for c in range(PROJ_PASSES):
+                k_pass = u * PROJ_PASSES + c
+                nc.tensor.matmul_mx(
+                    out=p_sum[h][:],
+                    lhsT=rgb_codes[:, k_pass, :].bitcast(FP8X4),
+                    lhsT_scale=rgb_scales[:, k_pass, :],
+                    rhs=proj_codes[:, c, :].bitcast(FP8X4),
+                    rhs_scale=proj_scales[:, c, :],
+                    start=(k_pass == 0),
+                    stop=(k_pass == D // K_PASS - 1),
+                )
+
+        def finish_head(h):
+            squares = tail.tile([T, DH], BF16, name="squares")
+            sum_sq = tail.tile([T, 1], F32, name="sum_sq")
+            nc.scalar.activation(out=squares[:], in_=p_sum[h][:], func=ACT.Square, accum_out=sum_sq[:])
+            floored = tail.tile([T, 1], F32, name="floored")
+            nc.vector.tensor_scalar_max(out=floored[:], in0=sum_sq[:], scalar1=EPS * EPS)
+            inv_sum_sq = tail.tile([T, 1], F32, name="inv_sum_sq")
+            nc.vector.reciprocal(out=inv_sum_sq[:], in_=floored[:])
+            inv_norm = tail.tile([T, 1], F32, name="inv_norm")
+            nc.scalar.sqrt(out=inv_norm[:], in_=inv_sum_sq[:])
+
+            o_bf16 = tail.tile([T, DH], BF16, name="o_bf16")
+            nc.scalar.activation(out=o_bf16[:], in_=p_sum[h][:], func=ACT.Copy, scale=inv_norm[:])
+            o_f32 = tail.tile([T, DH], F32, name="o_f32")
+            nc.scalar.activation(out=o_f32[:], in_=p_sum[h][:], func=ACT.Copy, scale=inv_norm[:])
+            nc.scalar.dma_start(out=out_0[0, h, :, :], in_=o_f32[:])
+
+            o_t = psum.tile([P, PACK, T], BF16, name="o_t")
+            for j in range(PACK):
+                nc.tensor.transpose(o_t[:, j, :], o_bf16[:, j * P : (j + 1) * P], identity[:])
+            o_grouped = tail.tile([P, T, PACK], BF16, name="o_grouped", align_bytes=64)
+            nc.scalar.copy(out=o_grouped[:], in_=o_t[:].rearrange("p j t -> p t j"))
+            o_codes = tail.tile([P, T], U32, name="o_codes", align_bytes=64)
+            o_scales = tail.tile([P, T], U8, name="o_scales", align_bytes=64)
+            nc.vector.quantize_mx(
+                out=o_codes[:].bitcast(FP8X4),
+                scales=o_scales[:],
+                in_=o_grouped[:].rearrange("p t j -> p (t j)"),
+            )
+            q_sum = psum.tile([T, DH], F32, name="q_sum")
+            nc.tensor.matmul_mx(
+                out=q_sum[:],
+                lhsT=o_codes[:].bitcast(FP8X4),
+                lhsT_scale=o_scales[:],
+                rhs=atte_codes[:, h, :].bitcast(FP8X4),
+                rhs_scale=atte_scales[:, h, :],
+                start=True,
+                stop=True,
+            )
+            q_f32 = tail.tile([T, DH], F32, name="q_f32")
+            nc.scalar.copy(out=q_f32[:], in_=q_sum[:])
+            nc.scalar.dma_start(out=out_1[0, h, :, :], in_=q_f32[:])
+
+        regrouped = None
+        for h in range(H):
+            for u in range(PROJ_LOADS):
+                if h == 0 and u % PROJ_LOADS_PER_RGB_LOAD == 0:
+                    r = u // PROJ_LOADS_PER_RGB_LOAD
+                    rgb_rows = rgb[0, r * RGB_PASSES * K_PASS : (r + 1) * RGB_PASSES * K_PASS, :]
+                    rgb_grouped = load_and_regroup(
+                        nc,
+                        raw_pool,
+                        grouped_pool,
+                        rgb_rows.rearrange("(c p j) t -> p c j t", c=RGB_PASSES, p=P, j=PACK),
+                        RGB_PASSES,
+                        T,
+                        "rgb",
+                    )
+                proj_rows = rgb_proj[h, u * PROJ_PASSES * K_PASS : (u + 1) * PROJ_PASSES * K_PASS, :]
+                proj_grouped = load_and_regroup(
+                    nc,
+                    raw_pool,
+                    grouped_pool,
+                    proj_rows.rearrange("(c p j) f -> p c j f", c=PROJ_PASSES, p=P, j=PACK),
+                    PROJ_PASSES,
+                    DH,
+                    "proj",
+                )
+                if h == 0 and u % PROJ_LOADS_PER_RGB_LOAD == 0:
+                    first = r * RGB_PASSES
+                    quantise(
+                        nc,
+                        rgb_grouped,
+                        rgb_codes[:, first : first + RGB_PASSES, :].rearrange("p c t -> p (c t)"),
+                        rgb_scales[:, first : first + RGB_PASSES, :].rearrange("p c t -> p (c t)"),
+                    )
+                if regrouped is not None:
+                    quantise_and_multiply(*regrouped)
+                    if regrouped[1] == PROJ_LOADS - 1:
+                        finish_head(regrouped[0])
+                regrouped = (h, u, proj_grouped)
+            if h == 0:
+                atte_grouped = load_and_regroup(
+                    nc,
+                    raw_pool,
+                    grouped_pool,
+                    atte_w.rearrange("h (j p) n -> p h j n", p=P),
+                    H,
+                    DH,
+                    "proj",
+                )
+                quantise(
+                    nc,
+                    atte_grouped,
+                    atte_codes[:].rearrange("p h n -> p (h n)"),
+                    atte_scales[:].rearrange("p h n -> p (h n)"),
+                )
+        quantise_and_multiply(*regrouped)
+        finish_head(regrouped[0])

@@ -59,6 +59,7 @@ def tile_mca_pa_k_kernel(tc, rgb, rgb_proj, atte_w, out_0, out_1):
         tail = ctx.enter_context(tc.tile_pool(name="tail", bufs=2))
         sums = ctx.enter_context(tc.psum_pool(name="sums", bufs=1))
         psum = ctx.enter_context(tc.psum_pool(name="psum", bufs=2))
+        ctx.enter_context(tc.manual_schedule())
 
         one = keep.tile([P, 1], F32, name="one")
         nc.vector.memset(one[:], 1.0)
@@ -96,55 +97,74 @@ def tile_mca_pa_k_kernel(tc, rgb, rgb_proj, atte_w, out_0, out_1):
                     stop=(k_pass == D // K_PASS - 1),
                 )
 
-        def finish_head(h):
+        def finish_steps(h):
             squares = tail.tile([T, DH], BF16, name="squares")
             sum_sq = tail.tile([T, 1], F32, name="sum_sq")
-            nc.scalar.activation(out=squares[:], in_=p_sum[h][:], func=ACT.Square, accum_out=sum_sq[:])
             floored = tail.tile([T, 1], F32, name="floored")
-            nc.vector.tensor_scalar_max(out=floored[:], in0=sum_sq[:], scalar1=EPS * EPS)
             inv_sum_sq = tail.tile([T, 1], F32, name="inv_sum_sq")
-            nc.vector.reciprocal(out=inv_sum_sq[:], in_=floored[:])
             inv_norm = tail.tile([T, 1], F32, name="inv_norm")
-            nc.scalar.sqrt(out=inv_norm[:], in_=inv_sum_sq[:])
-
             o_bf16 = tail.tile([T, DH], BF16, name="o_bf16")
-            nc.scalar.activation(out=o_bf16[:], in_=p_sum[h][:], func=ACT.Copy, scale=inv_norm[:])
             o_f32 = tail.tile([T, DH], F32, name="o_f32")
-            nc.scalar.activation(out=o_f32[:], in_=p_sum[h][:], func=ACT.Copy, scale=inv_norm[:])
-            nc.scalar.dma_start(out=out_0[0, h, :, :], in_=o_f32[:])
-
             o_t = psum.tile([P, PACK, T], BF16, name="o_t")
-            for j in range(PACK):
-                nc.tensor.transpose(o_t[:, j, :], o_bf16[:, j * P : (j + 1) * P], identity[:])
             o_grouped = tail.tile([P, T, PACK], BF16, name="o_grouped", align_bytes=64)
-            nc.scalar.copy(out=o_grouped[:], in_=o_t[:].rearrange("p j t -> p t j"))
             o_codes = tail.tile([P, T], U32, name="o_codes", align_bytes=64)
             o_scales = tail.tile([P, T], U8, name="o_scales", align_bytes=64)
-            nc.vector.quantize_mx(
-                out=o_codes[:].bitcast(FP8X4),
-                scales=o_scales[:],
-                in_=o_grouped[:].rearrange("p t j -> p (t j)"),
-            )
             q_sum = psum.tile([T, DH], F32, name="q_sum")
-            nc.tensor.matmul_mx(
-                out=q_sum[:],
-                lhsT=o_codes[:].bitcast(FP8X4),
-                lhsT_scale=o_scales[:],
-                rhs=atte_codes[:, h, :].bitcast(FP8X4),
-                rhs_scale=atte_scales[:, h, :],
-                start=True,
-                stop=True,
-            )
             q_f32 = tail.tile([T, DH], F32, name="q_f32")
-            nc.scalar.copy(out=q_f32[:], in_=q_sum[:])
-            nc.scalar.dma_start(out=out_1[0, h, :, :], in_=q_f32[:])
+
+            def sum_squares():
+                nc.scalar.activation(out=squares[:], in_=p_sum[h][:], func=ACT.Square, accum_out=sum_sq[:])
+
+            def invert():
+                nc.vector.tensor_scalar_max(out=floored[:], in0=sum_sq[:], scalar1=EPS * EPS)
+                nc.vector.reciprocal(out=inv_sum_sq[:], in_=floored[:])
+
+            def normalise():
+                nc.scalar.sqrt(out=inv_norm[:], in_=inv_sum_sq[:])
+                nc.scalar.activation(out=o_bf16[:], in_=p_sum[h][:], func=ACT.Copy, scale=inv_norm[:])
+                nc.scalar.activation(out=o_f32[:], in_=p_sum[h][:], func=ACT.Copy, scale=inv_norm[:])
+                nc.scalar.dma_start(out=out_0[0, h, :, :], in_=o_f32[:])
+
+            def transpose():
+                for j in range(PACK):
+                    nc.tensor.transpose(o_t[:, j, :], o_bf16[:, j * P : (j + 1) * P], identity[:])
+
+            def regroup():
+                nc.vector.tensor_copy(out=o_grouped[:], in_=o_t[:].rearrange("p j t -> p t j"))
+
+            def quantise_o():
+                nc.vector.quantize_mx(
+                    out=o_codes[:].bitcast(FP8X4),
+                    scales=o_scales[:],
+                    in_=o_grouped[:].rearrange("p t j -> p (t j)"),
+                )
+
+            def multiply():
+                nc.tensor.matmul_mx(
+                    out=q_sum[:],
+                    lhsT=o_codes[:].bitcast(FP8X4),
+                    lhsT_scale=o_scales[:],
+                    rhs=atte_codes[:, h, :].bitcast(FP8X4),
+                    rhs_scale=atte_scales[:, h, :],
+                    start=True,
+                    stop=True,
+                )
+
+            def store_q():
+                nc.scalar.copy(out=q_f32[:], in_=q_sum[:])
+                nc.scalar.dma_start(out=out_1[0, h, :, :], in_=q_f32[:])
+
+            return [sum_squares, invert, normalise, transpose, regroup, quantise_o, multiply, store_q]
 
         regrouped = None
+        steps = []
         for h in range(H):
             for u in range(PROJ_LOADS):
-                if h == 0 and u % PROJ_LOADS_PER_RGB_LOAD == 0:
-                    r = u // PROJ_LOADS_PER_RGB_LOAD
-                    rgb_rows = rgb[0, r * RGB_PASSES * K_PASS : (r + 1) * RGB_PASSES * K_PASS, :]
+                new_rgb = h == 0 and u % PROJ_LOADS_PER_RGB_LOAD == 0
+                new_atte = h == 1 and u == 0
+                if new_rgb:
+                    first = (u // PROJ_LOADS_PER_RGB_LOAD) * RGB_PASSES
+                    rgb_rows = rgb[0, first * K_PASS : (first + RGB_PASSES) * K_PASS, :]
                     rgb_grouped = load_and_regroup(
                         nc,
                         raw_pool,
@@ -153,6 +173,10 @@ def tile_mca_pa_k_kernel(tc, rgb, rgb_proj, atte_w, out_0, out_1):
                         RGB_PASSES,
                         T,
                         "rgb",
+                    )
+                if new_atte:
+                    atte_grouped = load_and_regroup(
+                        nc, raw_pool, grouped_pool, atte_w.rearrange("h (j p) n -> p h j n", p=P), H, DH, "proj"
                     )
                 proj_rows = rgb_proj[h, u * PROJ_PASSES * K_PASS : (u + 1) * PROJ_PASSES * K_PASS, :]
                 proj_grouped = load_and_regroup(
@@ -164,34 +188,28 @@ def tile_mca_pa_k_kernel(tc, rgb, rgb_proj, atte_w, out_0, out_1):
                     DH,
                     "proj",
                 )
-                if h == 0 and u % PROJ_LOADS_PER_RGB_LOAD == 0:
-                    first = r * RGB_PASSES
+                if new_rgb:
                     quantise(
                         nc,
                         rgb_grouped,
                         rgb_codes[:, first : first + RGB_PASSES, :].rearrange("p c t -> p (c t)"),
                         rgb_scales[:, first : first + RGB_PASSES, :].rearrange("p c t -> p (c t)"),
                     )
+                if new_atte:
+                    quantise(
+                        nc,
+                        atte_grouped,
+                        atte_codes[:].rearrange("p h n -> p (h n)"),
+                        atte_scales[:].rearrange("p h n -> p (h n)"),
+                    )
+                if steps:
+                    steps[0]()
+                    steps = steps[1:]
                 if regrouped is not None:
                     quantise_and_multiply(*regrouped)
                     if regrouped[1] == PROJ_LOADS - 1:
-                        finish_head(regrouped[0])
+                        steps = finish_steps(regrouped[0])
                 regrouped = (h, u, proj_grouped)
-            if h == 0:
-                atte_grouped = load_and_regroup(
-                    nc,
-                    raw_pool,
-                    grouped_pool,
-                    atte_w.rearrange("h (j p) n -> p h j n", p=P),
-                    H,
-                    DH,
-                    "proj",
-                )
-                quantise(
-                    nc,
-                    atte_grouped,
-                    atte_codes[:].rearrange("p h n -> p (h n)"),
-                    atte_scales[:].rearrange("p h n -> p (h n)"),
-                )
         quantise_and_multiply(*regrouped)
-        finish_head(regrouped[0])
+        for step in finish_steps(regrouped[0]):
+            step()

@@ -32,12 +32,15 @@ def load_and_regroup(nc, raw_pool, grouped_pool, source, passes, width, label):
     grouped = grouped_pool.tile(
         [P, passes, width, PACK], BF16, name="grouped_" + label, tag="grouped_" + label, align_bytes=64
     )
+    scalar_columns = passes * width // 2
     for c in range(passes):
-        copy = nc.scalar.copy if c < passes // 2 else nc.vector.tensor_copy
-        copy(
-            out=grouped[:, c, :, :].rearrange("p (g i) j -> p g j i", i=RUN),
-            in_=raw[:, c, :, :].rearrange("p j (g i) -> p g j i", i=RUN),
-        )
+        split = min(max(scalar_columns - c * width, 0), width)
+        for copy, lo, hi in ((nc.scalar.copy, 0, split), (nc.vector.tensor_copy, split, width)):
+            if lo < hi:
+                copy(
+                    out=grouped[:, c, lo:hi, :].rearrange("p (g i) j -> p g j i", i=RUN),
+                    in_=raw[:, c, :, lo:hi].rearrange("p j (g i) -> p g j i", i=RUN),
+                )
     return grouped
 
 
@@ -55,6 +58,7 @@ def tile_mca_pa_k_kernel(tc, rgb, rgb_proj, atte_w, out_0, out_1):
         keep = ctx.enter_context(tc.tile_pool(name="keep", bufs=1))
         raw_pool = ctx.enter_context(tc.tile_pool(name="raw", bufs=8))
         grouped_pool = ctx.enter_context(tc.tile_pool(name="grouped", bufs=3))
+        atte_pool = ctx.enter_context(tc.tile_pool(name="atte", bufs=1))
         mx_pool = ctx.enter_context(tc.tile_pool(name="mx", bufs=3))
         tail = ctx.enter_context(tc.tile_pool(name="tail", bufs=2))
         sums = ctx.enter_context(tc.psum_pool(name="sums", bufs=1))
@@ -75,6 +79,8 @@ def tile_mca_pa_k_kernel(tc, rgb, rgb_proj, atte_w, out_0, out_1):
         atte_scales = keep.tile([P, H, DH], U8, name="atte_scales", align_bytes=64)
 
         p_sum = [sums.tile([T, DH], F32, name="p_sum%d" % h) for h in range(H)]
+        o_f32 = [keep.tile([T, DH], F32, name="o_f32_%d" % h) for h in range(H)]
+        q_f32 = [keep.tile([T, DH], F32, name="q_f32_%d" % h) for h in range(H)]
 
         def quantise_and_multiply(h, u, grouped):
             proj_codes = mx_pool.tile([P, PROJ_PASSES, DH], U32, name="proj_codes", align_bytes=64)
@@ -104,13 +110,11 @@ def tile_mca_pa_k_kernel(tc, rgb, rgb_proj, atte_w, out_0, out_1):
             inv_sum_sq = tail.tile([T, 1], F32, name="inv_sum_sq")
             inv_norm = tail.tile([T, 1], F32, name="inv_norm")
             o_bf16 = tail.tile([T, DH], BF16, name="o_bf16")
-            o_f32 = tail.tile([T, DH], F32, name="o_f32")
             o_t = psum.tile([P, PACK, T], BF16, name="o_t")
             o_grouped = tail.tile([P, T, PACK], BF16, name="o_grouped", align_bytes=64)
             o_codes = tail.tile([P, T], U32, name="o_codes", align_bytes=64)
             o_scales = tail.tile([P, T], U8, name="o_scales", align_bytes=64)
             q_sum = psum.tile([T, DH], F32, name="q_sum")
-            q_f32 = tail.tile([T, DH], F32, name="q_f32")
 
             def sum_squares():
                 nc.scalar.activation(out=squares[:], in_=p_sum[h][:], func=ACT.Square, accum_out=sum_sq[:])
@@ -122,8 +126,7 @@ def tile_mca_pa_k_kernel(tc, rgb, rgb_proj, atte_w, out_0, out_1):
             def normalise():
                 nc.scalar.sqrt(out=inv_norm[:], in_=inv_sum_sq[:])
                 nc.scalar.activation(out=o_bf16[:], in_=p_sum[h][:], func=ACT.Copy, scale=inv_norm[:])
-                nc.scalar.activation(out=o_f32[:], in_=p_sum[h][:], func=ACT.Copy, scale=inv_norm[:])
-                nc.scalar.dma_start(out=out_0[0, h, :, :], in_=o_f32[:])
+                nc.scalar.activation(out=o_f32[h][:], in_=p_sum[h][:], func=ACT.Copy, scale=inv_norm[:])
 
             def transpose():
                 for j in range(PACK):
@@ -150,18 +153,16 @@ def tile_mca_pa_k_kernel(tc, rgb, rgb_proj, atte_w, out_0, out_1):
                     stop=True,
                 )
 
-            def store_q():
-                nc.scalar.copy(out=q_f32[:], in_=q_sum[:])
-                nc.scalar.dma_start(out=out_1[0, h, :, :], in_=q_f32[:])
+            def copy_q():
+                nc.scalar.copy(out=q_f32[h][:], in_=q_sum[:])
 
-            return [sum_squares, invert, normalise, transpose, regroup, quantise_o, multiply, store_q]
+            return [sum_squares, invert, normalise, transpose, regroup, quantise_o, multiply, copy_q]
 
-        regrouped = None
         steps = []
         for h in range(H):
+            regrouped = None
             for u in range(PROJ_LOADS):
                 new_rgb = h == 0 and u % PROJ_LOADS_PER_RGB_LOAD == 0
-                new_atte = h == 1 and u == 0
                 if new_rgb:
                     first = (u // PROJ_LOADS_PER_RGB_LOAD) * RGB_PASSES
                     rgb_rows = rgb[0, first * K_PASS : (first + RGB_PASSES) * K_PASS, :]
@@ -173,10 +174,6 @@ def tile_mca_pa_k_kernel(tc, rgb, rgb_proj, atte_w, out_0, out_1):
                         RGB_PASSES,
                         T,
                         "rgb",
-                    )
-                if new_atte:
-                    atte_grouped = load_and_regroup(
-                        nc, raw_pool, grouped_pool, atte_w.rearrange("h (j p) n -> p h j n", p=P), H, DH, "proj"
                     )
                 proj_rows = rgb_proj[h, u * PROJ_PASSES * K_PASS : (u + 1) * PROJ_PASSES * K_PASS, :]
                 proj_grouped = load_and_regroup(
@@ -195,21 +192,20 @@ def tile_mca_pa_k_kernel(tc, rgb, rgb_proj, atte_w, out_0, out_1):
                         rgb_codes[:, first : first + RGB_PASSES, :].rearrange("p c t -> p (c t)"),
                         rgb_scales[:, first : first + RGB_PASSES, :].rearrange("p c t -> p (c t)"),
                     )
-                if new_atte:
-                    quantise(
-                        nc,
-                        atte_grouped,
-                        atte_codes[:].rearrange("p h n -> p (h n)"),
-                        atte_scales[:].rearrange("p h n -> p (h n)"),
-                    )
                 if steps:
                     steps[0]()
                     steps = steps[1:]
                 if regrouped is not None:
-                    quantise_and_multiply(*regrouped)
-                    if regrouped[1] == PROJ_LOADS - 1:
-                        steps = finish_steps(regrouped[0])
-                regrouped = (h, u, proj_grouped)
-        quantise_and_multiply(*regrouped)
-        for step in finish_steps(regrouped[0]):
+                    quantise_and_multiply(h, u - 1, regrouped)
+                regrouped = proj_grouped
+            quantise_and_multiply(h, PROJ_LOADS - 1, regrouped)
+            atte_grouped = load_and_regroup(
+                nc, atte_pool, atte_pool, atte_w[h : h + 1, :, :].rearrange("c (j p) n -> p c j n", p=P), 1, DH, "atte"
+            )
+            quantise(nc, atte_grouped, atte_codes[:, h, :], atte_scales[:, h, :])
+            steps = finish_steps(h)
+        for step in steps:
             step()
+        for h in range(H):
+            nc.sync.dma_start(out=out_0[0, h, :, :], in_=o_f32[h][:])
+            nc.sync.dma_start(out=out_1[0, h, :, :], in_=q_f32[h][:])

@@ -9,18 +9,20 @@ U32 = mybir.dt.uint32
 U8 = mybir.dt.uint8
 FP8X4 = mybir.dt.float8_e4m3fn_x4
 ACT = mybir.ActivationFunctionType
+ALU = mybir.AluOpType
 
 P = 128
 PACK = 4
 K_PASS = P * PACK
 
 D, T, H, DH = 16384, 128, 2, 512
+HALF = DH // 2
 EPS = 1e-12
+PASSES = D // K_PASS
 
-PROJ_PASSES = 2
-RGB_PASSES = 4
-PROJ_LOADS = D // (PROJ_PASSES * K_PASS)
-PROJ_LOADS_PER_RGB_LOAD = RGB_PASSES // PROJ_PASSES
+RGB_LOADS = [2, 2] + [4] * 7
+PROJ_LOADS = [[1, 1] + [2] * 15, [2] * 15 + [1, 1]]
+ATTE_SLOT = 2
 RUN = 4
 
 FLOPS = 2 * H * T * D * DH + 2 * H * T * DH * DH
@@ -44,96 +46,120 @@ def load_and_regroup(nc, raw_pool, grouped_pool, source, passes, width, label):
     return grouped
 
 
-def quantise(nc, grouped, codes, scales):
-    nc.vector.quantize_mx(
-        out=codes.bitcast(FP8X4),
-        scales=scales,
-        in_=grouped[:].rearrange("p c w j -> p (c w j)"),
-    )
-
-
 def tile_mca_pa_k_kernel(tc, rgb, rgb_proj, atte_w, out_0, out_1):
     nc = tc.nc
     with ExitStack() as ctx:
         keep = ctx.enter_context(tc.tile_pool(name="keep", bufs=1))
         raw_pool = ctx.enter_context(tc.tile_pool(name="raw", bufs=8))
         grouped_pool = ctx.enter_context(tc.tile_pool(name="grouped", bufs=3))
-        atte_pool = ctx.enter_context(tc.tile_pool(name="atte", bufs=1))
         mx_pool = ctx.enter_context(tc.tile_pool(name="mx", bufs=3))
         tail = ctx.enter_context(tc.tile_pool(name="tail", bufs=2))
-        sums = ctx.enter_context(tc.psum_pool(name="sums", bufs=1))
-        psum = ctx.enter_context(tc.psum_pool(name="psum", bufs=2))
+        sums = ctx.enter_context(tc.psum_pool(name="sums", bufs=2))
+        psum = ctx.enter_context(tc.psum_pool(name="psum", bufs=1))
         ctx.enter_context(tc.manual_schedule())
 
         one = keep.tile([P, 1], F32, name="one")
         nc.vector.memset(one[:], 1.0)
-        root_of_one = keep.tile([P, 1], F32, name="root_of_one")
-        nc.scalar.sqrt(out=root_of_one[:], in_=one[:])
+        warm = keep.tile([P, 1], F32, name="warm")
+        nc.scalar.activation(out=warm[:], in_=one[:], func=ACT.Abs_reciprocal_sqrt)
 
         identity = keep.tile([P, P], BF16, name="identity")
         make_identity(nc, identity[:])
 
-        rgb_codes = keep.tile([P, D // K_PASS, T], U32, name="rgb_codes", align_bytes=64)
-        rgb_scales = keep.tile([P, D // K_PASS, T], U8, name="rgb_scales", align_bytes=64)
+        rgb_codes = keep.tile([P, PASSES, T], U32, name="rgb_codes", align_bytes=64)
+        rgb_scales = keep.tile([P, PASSES, T], U8, name="rgb_scales", align_bytes=64)
         atte_codes = keep.tile([P, H, DH], U32, name="atte_codes", align_bytes=64)
         atte_scales = keep.tile([P, H, DH], U8, name="atte_scales", align_bytes=64)
 
-        p_sum = [sums.tile([T, DH], F32, name="p_sum%d" % h) for h in range(H)]
+        p_sum = [[sums.tile([T, HALF], F32, name="sum_%d" % b) for b in range(2)] for h in range(H)]
         o_f32 = [keep.tile([T, DH], F32, name="o_f32_%d" % h) for h in range(H)]
         q_f32 = [keep.tile([T, DH], F32, name="q_f32_%d" % h) for h in range(H)]
 
-        def quantise_and_multiply(h, u, grouped):
-            proj_codes = mx_pool.tile([P, PROJ_PASSES, DH], U32, name="proj_codes", align_bytes=64)
-            proj_scales = mx_pool.tile([P, PROJ_PASSES, DH], U8, name="proj_scales", align_bytes=64)
-            quantise(
-                nc,
-                grouped,
-                proj_codes[:].rearrange("p c w -> p (c w)"),
-                proj_scales[:].rearrange("p c w -> p (c w)"),
+        def finish_rgb(first, passes, grouped):
+            nc.vector.quantize_mx(
+                out=rgb_codes[:, first : first + passes, :].rearrange("p c t -> p (c t)").bitcast(FP8X4),
+                scales=rgb_scales[:, first : first + passes, :].rearrange("p c t -> p (c t)"),
+                in_=grouped[:].rearrange("p c t j -> p (c t j)"),
             )
-            for c in range(PROJ_PASSES):
-                k_pass = u * PROJ_PASSES + c
-                nc.tensor.matmul_mx(
-                    out=p_sum[h][:],
-                    lhsT=rgb_codes[:, k_pass, :].bitcast(FP8X4),
-                    lhsT_scale=rgb_scales[:, k_pass, :],
-                    rhs=proj_codes[:, c, :].bitcast(FP8X4),
-                    rhs_scale=proj_scales[:, c, :],
-                    start=(k_pass == 0),
-                    stop=(k_pass == D // K_PASS - 1),
-                )
+
+        def finish_atte(grouped):
+            nc.vector.quantize_mx(
+                out=atte_codes[:].rearrange("p h n -> p (h n)").bitcast(FP8X4),
+                scales=atte_scales[:].rearrange("p h n -> p (h n)"),
+                in_=grouped[:].rearrange("p h n j -> p (h n j)"),
+            )
+
+        def finish_proj(h, first, passes, grouped):
+            proj_codes = mx_pool.tile([P, passes, DH], U32, name="proj_codes", align_bytes=64)
+            proj_scales = mx_pool.tile([P, passes, DH], U8, name="proj_scales", align_bytes=64)
+            nc.vector.quantize_mx(
+                out=proj_codes[:].rearrange("p c w -> p (c w)").bitcast(FP8X4),
+                scales=proj_scales[:].rearrange("p c w -> p (c w)"),
+                in_=grouped[:].rearrange("p c w j -> p (c w j)"),
+            )
+            for c in range(passes):
+                k_pass = first + c
+                for b in range(2):
+                    nc.tensor.matmul_mx(
+                        out=p_sum[h][b][:],
+                        lhsT=rgb_codes[:, k_pass, :].bitcast(FP8X4),
+                        lhsT_scale=rgb_scales[:, k_pass, :],
+                        rhs=proj_codes[:, c, b * HALF : (b + 1) * HALF].bitcast(FP8X4),
+                        rhs_scale=proj_scales[:, c, b * HALF : (b + 1) * HALF],
+                        start=(k_pass == 0),
+                        stop=(k_pass == PASSES - 1),
+                    )
 
         def finish_steps(h):
-            squares = tail.tile([T, DH], BF16, name="squares")
-            sum_sq = tail.tile([T, 1], F32, name="sum_sq")
+            squares = tail.tile([T, HALF], BF16, name="squares")
+            half_sum = tail.tile([T, 2], F32, name="half_sum")
             floored = tail.tile([T, 1], F32, name="floored")
-            inv_sum_sq = tail.tile([T, 1], F32, name="inv_sum_sq")
             inv_norm = tail.tile([T, 1], F32, name="inv_norm")
-            o_bf16 = tail.tile([T, DH], BF16, name="o_bf16")
+            o_bf16 = tail.tile([T, PACK, P], BF16, name="o_bf16")
             o_t = psum.tile([P, PACK, T], BF16, name="o_t")
             o_grouped = tail.tile([P, T, PACK], BF16, name="o_grouped", align_bytes=64)
             o_codes = tail.tile([P, T], U32, name="o_codes", align_bytes=64)
             o_scales = tail.tile([P, T], U8, name="o_scales", align_bytes=64)
-            q_sum = psum.tile([T, DH], F32, name="q_sum")
+            q_sum = []
 
             def sum_squares():
-                nc.scalar.activation(out=squares[:], in_=p_sum[h][:], func=ACT.Square, accum_out=sum_sq[:])
+                for b in range(2):
+                    nc.scalar.activation(
+                        out=squares[:], in_=p_sum[h][b][:], func=ACT.Square, accum_out=half_sum[:, b : b + 1]
+                    )
 
             def invert():
-                nc.vector.tensor_scalar_max(out=floored[:], in0=sum_sq[:], scalar1=EPS * EPS)
-                nc.vector.reciprocal(out=inv_sum_sq[:], in_=floored[:])
+                nc.vector.tensor_scalar(
+                    out=floored[:],
+                    in0=half_sum[:, 0:1],
+                    scalar1=half_sum[:, 1:2],
+                    scalar2=EPS * EPS,
+                    op0=ALU.add,
+                    op1=ALU.max,
+                )
+                nc.scalar.activation(out=inv_norm[:], in_=floored[:], func=ACT.Abs_reciprocal_sqrt)
 
             def normalise():
-                nc.scalar.sqrt(out=inv_norm[:], in_=inv_sum_sq[:])
-                nc.scalar.activation(out=o_bf16[:], in_=p_sum[h][:], func=ACT.Copy, scale=inv_norm[:])
-                nc.scalar.activation(out=o_f32[h][:], in_=p_sum[h][:], func=ACT.Copy, scale=inv_norm[:])
+                nc.scalar.activation(
+                    out=o_bf16[:, :, : P // 2],
+                    in_=p_sum[h][0][:].rearrange("t (q j) -> t j q", j=PACK),
+                    func=ACT.Copy,
+                    scale=inv_norm[:],
+                )
+                nc.vector.tensor_scalar_mul(
+                    out=o_bf16[:, :, P // 2 :],
+                    in0=p_sum[h][1][:].rearrange("t (q j) -> t j q", j=PACK),
+                    scalar1=inv_norm[:],
+                )
+                nc.scalar.activation(out=o_f32[h][:, :HALF], in_=p_sum[h][0][:], func=ACT.Copy, scale=inv_norm[:])
+                nc.vector.tensor_scalar_mul(out=o_f32[h][:, HALF:], in0=p_sum[h][1][:], scalar1=inv_norm[:])
 
             def transpose():
                 for j in range(PACK):
-                    nc.tensor.transpose(o_t[:, j, :], o_bf16[:, j * P : (j + 1) * P], identity[:])
+                    nc.tensor.matmul(o_t[:, j, :], lhsT=o_bf16[:, j, :], rhs=identity[:], start=True, stop=True)
 
             def regroup():
-                nc.vector.tensor_copy(out=o_grouped[:], in_=o_t[:].rearrange("p j t -> p t j"))
+                nc.scalar.copy(out=o_grouped[:], in_=o_t[:].rearrange("p j t -> p t j"))
 
             def quantise_o():
                 nc.vector.quantize_mx(
@@ -143,69 +169,66 @@ def tile_mca_pa_k_kernel(tc, rgb, rgb_proj, atte_w, out_0, out_1):
                 )
 
             def multiply():
-                nc.tensor.matmul_mx(
-                    out=q_sum[:],
-                    lhsT=o_codes[:].bitcast(FP8X4),
-                    lhsT_scale=o_scales[:],
-                    rhs=atte_codes[:, h, :].bitcast(FP8X4),
-                    rhs_scale=atte_scales[:, h, :],
-                    start=True,
-                    stop=True,
-                )
+                for b in range(2):
+                    half = sums.tile([T, HALF], F32, name="q_half", tag="sum_%d" % b)
+                    nc.tensor.matmul_mx(
+                        out=half[:],
+                        lhsT=o_codes[:].bitcast(FP8X4),
+                        lhsT_scale=o_scales[:],
+                        rhs=atte_codes[:, h, b * HALF : (b + 1) * HALF].bitcast(FP8X4),
+                        rhs_scale=atte_scales[:, h, b * HALF : (b + 1) * HALF],
+                        start=True,
+                        stop=True,
+                    )
+                    q_sum.append(half)
 
             def copy_q():
-                nc.scalar.copy(out=q_f32[h][:], in_=q_sum[:])
+                nc.scalar.copy(out=q_f32[h][:, :HALF], in_=q_sum[0][:])
+                nc.vector.tensor_copy(out=q_f32[h][:, HALF:], in_=q_sum[1][:])
 
             return [sum_squares, invert, normalise, transpose, regroup, quantise_o, multiply, copy_q]
 
-        steps = []
+        stream = []
+        rgb_sizes = RGB_LOADS
+        rgb_passes = 0
         for h in range(H):
-            regrouped = None
-            for u in range(PROJ_LOADS):
-                new_rgb = h == 0 and u % PROJ_LOADS_PER_RGB_LOAD == 0
-                if new_rgb:
-                    first = (u // PROJ_LOADS_PER_RGB_LOAD) * RGB_PASSES
-                    rgb_rows = rgb[0, first * K_PASS : (first + RGB_PASSES) * K_PASS, :]
-                    rgb_grouped = load_and_regroup(
-                        nc,
-                        raw_pool,
-                        grouped_pool,
-                        rgb_rows.rearrange("(c p j) t -> p c j t", c=RGB_PASSES, p=P, j=PACK),
-                        RGB_PASSES,
-                        T,
-                        "rgb",
-                    )
-                proj_rows = rgb_proj[h, u * PROJ_PASSES * K_PASS : (u + 1) * PROJ_PASSES * K_PASS, :]
-                proj_grouped = load_and_regroup(
-                    nc,
-                    raw_pool,
-                    grouped_pool,
-                    proj_rows.rearrange("(c p j) f -> p c j f", c=PROJ_PASSES, p=P, j=PACK),
-                    PROJ_PASSES,
-                    DH,
-                    "proj",
-                )
-                if new_rgb:
-                    quantise(
-                        nc,
-                        rgb_grouped,
-                        rgb_codes[:, first : first + RGB_PASSES, :].rearrange("p c t -> p (c t)"),
-                        rgb_scales[:, first : first + RGB_PASSES, :].rearrange("p c t -> p (c t)"),
-                    )
-                if steps:
-                    steps[0]()
-                    steps = steps[1:]
-                if regrouped is not None:
-                    quantise_and_multiply(h, u - 1, regrouped)
-                regrouped = proj_grouped
-            quantise_and_multiply(h, PROJ_LOADS - 1, regrouped)
-            atte_grouped = load_and_regroup(
-                nc, atte_pool, atte_pool, atte_w[h : h + 1, :, :].rearrange("c (j p) n -> p c j n", p=P), 1, DH, "atte"
-            )
-            quantise(nc, atte_grouped, atte_codes[:, h, :], atte_scales[:, h, :])
-            steps = finish_steps(h)
+            first = 0
+            for u, passes in enumerate(PROJ_LOADS[h]):
+                while rgb_passes < first + passes:
+                    rows = rgb[0, rgb_passes * K_PASS : (rgb_passes + rgb_sizes[0]) * K_PASS, :]
+                    rows = rows.rearrange("(c p j) t -> p c j t", p=P, j=PACK)
+                    stream.append((finish_rgb, (rgb_passes, rgb_sizes[0]), rows, rgb_sizes[0], T, "rgb"))
+                    rgb_passes += rgb_sizes[0]
+                    rgb_sizes = rgb_sizes[1:]
+                if h == H - 1 and u == ATTE_SLOT:
+                    rows = atte_w.rearrange("h (p j) n -> p h j n", p=P, j=PACK)
+                    stream.append((finish_atte, (), rows, H, DH, "proj"))
+                rows = rgb_proj[h, first * K_PASS : (first + passes) * K_PASS, :]
+                rows = rows.rearrange("(c p j) f -> p c j f", p=P, j=PACK)
+                stream.append((finish_proj, (h, first, passes), rows, passes, DH, "proj"))
+                first += passes
+
+        steps = []
+        waiting = None
+        for entry in stream + [None]:
+            grouped = None
+            if entry is not None:
+                grouped = load_and_regroup(nc, raw_pool, grouped_pool, entry[2], entry[3], entry[4], entry[5])
+            if steps:
+                steps[0]()
+                steps = steps[1:]
+            if waiting is not None:
+                finish, args, tile_grouped = waiting
+                finish(*args, tile_grouped)
+                if finish is finish_proj and args[1] + args[2] == PASSES:
+                    steps = finish_steps(args[0])
+            if entry is not None:
+                waiting = (entry[0], entry[1], grouped)
         for step in steps:
             step()
-        for h in range(H):
-            nc.sync.dma_start(out=out_0[0, h, :, :], in_=o_f32[h][:])
-            nc.sync.dma_start(out=out_1[0, h, :, :], in_=q_f32[h][:])
+        nc.sync.dma_start(out=out_0[0, 0, :, :], in_=o_f32[0][:])
+        nc.sync.dma_start(out=out_1[0, 0, :, :], in_=q_f32[0][:])
+        nc.sync.dma_start(out=out_0[0, 1, :, :], in_=o_f32[1][:])
+        for b in range(2):
+            cols = slice(b * HALF, (b + 1) * HALF)
+            nc.sync.dma_start(out=out_1[0, 1, :, cols], in_=q_f32[1][:, cols])

@@ -23,7 +23,7 @@ PASSES = D // K_PASS
 RGB_LOADS = [2, 2] + [4] * 7
 PROJ_LOADS = [[1, 1] + [2] * 15, [2] * 15 + [1, 1]]
 ATTE_SLOT = 2
-RUN = 4
+RUN = 8
 
 FLOPS = 2 * H * T * D * DH + 2 * H * T * DH * DH
 

@@ -9,7 +9,6 @@ U32 = mybir.dt.uint32
 U8 = mybir.dt.uint8
 FP8X4 = mybir.dt.float8_e4m3fn_x4
 ACT = mybir.ActivationFunctionType
-ALU = mybir.AluOpType
 
 P = 128
 PACK = 4
@@ -22,28 +21,28 @@ PASSES = D // K_PASS
 
 RGB_LOADS = [2, 2] + [4] * 7
 PROJ_LOADS = [[1, 1] + [2] * 15, [2] * 15 + [1, 1]]
-ATTE_SLOT = 2
 RUN = 8
 
 FLOPS = 2 * H * T * D * DH + 2 * H * T * DH * DH
 
 
-def load_and_regroup(nc, raw_pool, grouped_pool, source, passes, width, label):
-    raw = raw_pool.tile([P, passes, PACK, width], BF16, name="raw_" + label, tag="raw_" + label)
-    nc.sync.dma_start(out=raw[:], in_=source)
-    grouped = grouped_pool.tile(
-        [P, passes, width, PACK], BF16, name="grouped_" + label, tag="grouped_" + label, align_bytes=64
+def interleave(copy, raw, grouped):
+    copy(
+        out=grouped.rearrange("p c (g i) j -> p c g j i", i=RUN),
+        in_=raw.rearrange("p c j (g i) -> p c g j i", i=RUN),
     )
-    scalar_columns = passes * width // 2
-    for c in range(passes):
-        split = min(max(scalar_columns - c * width, 0), width)
-        for copy, lo, hi in ((nc.scalar.copy, 0, split), (nc.vector.tensor_copy, split, width)):
-            if lo < hi:
-                copy(
-                    out=grouped[:, c, lo:hi, :].rearrange("p (g i) j -> p g j i", i=RUN),
-                    in_=raw[:, c, :, lo:hi].rearrange("p j (g i) -> p g j i", i=RUN),
-                )
-    return grouped
+
+
+def regroup(nc, raw, grouped):
+    passes, width = raw.shape[1], raw.shape[3]
+    if passes > 1:
+        half = passes // 2
+        interleave(nc.scalar.copy, raw[:, :half, :, :], grouped[:, :half, :, :])
+        interleave(nc.vector.tensor_copy, raw[:, half:, :, :], grouped[:, half:, :, :])
+    else:
+        half = width // 2
+        interleave(nc.scalar.copy, raw[:, :, :, :half], grouped[:, :, :half, :])
+        interleave(nc.vector.tensor_copy, raw[:, :, :, half:], grouped[:, :, half:, :])
 
 
 def tile_mca_pa_k_kernel(tc, rgb, rgb_proj, atte_w, out_0, out_1):
@@ -53,9 +52,7 @@ def tile_mca_pa_k_kernel(tc, rgb, rgb_proj, atte_w, out_0, out_1):
         raw_pool = ctx.enter_context(tc.tile_pool(name="raw", bufs=8))
         grouped_pool = ctx.enter_context(tc.tile_pool(name="grouped", bufs=3))
         mx_pool = ctx.enter_context(tc.tile_pool(name="mx", bufs=3))
-        tail = ctx.enter_context(tc.tile_pool(name="tail", bufs=2))
-        sums = ctx.enter_context(tc.psum_pool(name="sums", bufs=2))
-        psum = ctx.enter_context(tc.psum_pool(name="psum", bufs=1))
+        sums = ctx.enter_context(tc.psum_pool(name="sums", bufs=1))
         ctx.enter_context(tc.manual_schedule())
 
         one = keep.tile([P, 1], F32, name="one")
@@ -71,9 +68,20 @@ def tile_mca_pa_k_kernel(tc, rgb, rgb_proj, atte_w, out_0, out_1):
         atte_codes = keep.tile([P, H, DH], U32, name="atte_codes", align_bytes=64)
         atte_scales = keep.tile([P, H, DH], U8, name="atte_scales", align_bytes=64)
 
-        p_sum = [[sums.tile([T, HALF], F32, name="sum_%d" % b) for b in range(2)] for h in range(H)]
+        p_sum = [sums.tile([T, DH], F32, name="p_sum%d" % h) for h in range(H)]
         o_f32 = [keep.tile([T, DH], F32, name="o_f32_%d" % h) for h in range(H)]
         q_f32 = [keep.tile([T, DH], F32, name="q_f32_%d" % h) for h in range(H)]
+        q_sum_0 = sums.tile([T, DH], F32, name="q_sum_0")
+        q_halves_1 = [sums.tile([T, HALF], F32, name="q_half_%d" % b) for b in range(2)]
+        squares = [keep.tile([T, DH], BF16, name="squares_%d" % h) for h in range(H)]
+        sum_sq = [keep.tile([T, 1], F32, name="sum_sq_%d" % h) for h in range(H)]
+        floored = [keep.tile([T, 1], F32, name="floored_%d" % h) for h in range(H)]
+        inv_norm = [keep.tile([T, 1], F32, name="inv_norm_%d" % h) for h in range(H)]
+        o_bf16 = [keep.tile([T, PACK, P], BF16, name="o_bf16_%d" % h) for h in range(H)]
+        o_t = [sums.tile([P, PACK, T], BF16, name="o_t_%d" % h) for h in range(H)]
+        o_grouped = [keep.tile([P, T, PACK], BF16, name="o_grouped_%d" % h, align_bytes=64) for h in range(H)]
+        o_codes = [keep.tile([P, T], U32, name="o_codes_%d" % h, align_bytes=64) for h in range(H)]
+        o_scales = [keep.tile([P, T], U8, name="o_scales_%d" % h, align_bytes=64) for h in range(H)]
 
         def finish_rgb(first, passes, grouped):
             nc.vector.quantize_mx(
@@ -82,127 +90,87 @@ def tile_mca_pa_k_kernel(tc, rgb, rgb_proj, atte_w, out_0, out_1):
                 in_=grouped[:].rearrange("p c t j -> p (c t j)"),
             )
 
-        def finish_atte(grouped):
+        def finish_atte(h, grouped):
             nc.vector.quantize_mx(
-                out=atte_codes[:].rearrange("p h n -> p (h n)").bitcast(FP8X4),
-                scales=atte_scales[:].rearrange("p h n -> p (h n)"),
-                in_=grouped[:].rearrange("p h n j -> p (h n j)"),
+                out=atte_codes[:, h, :].bitcast(FP8X4),
+                scales=atte_scales[:, h, :],
+                in_=grouped[:].rearrange("p c n j -> p (c n j)"),
             )
 
         def finish_proj(h, first, passes, grouped):
-            proj_codes = mx_pool.tile([P, passes, DH], U32, name="proj_codes", align_bytes=64)
-            proj_scales = mx_pool.tile([P, passes, DH], U8, name="proj_scales", align_bytes=64)
+            codes = mx_pool.tile([P, passes, DH], U32, name="proj_codes", align_bytes=64)
+            scales = mx_pool.tile([P, passes, DH], U8, name="proj_scales", align_bytes=64)
             nc.vector.quantize_mx(
-                out=proj_codes[:].rearrange("p c w -> p (c w)").bitcast(FP8X4),
-                scales=proj_scales[:].rearrange("p c w -> p (c w)"),
+                out=codes[:].rearrange("p c w -> p (c w)").bitcast(FP8X4),
+                scales=scales[:].rearrange("p c w -> p (c w)"),
                 in_=grouped[:].rearrange("p c w j -> p (c w j)"),
             )
             for c in range(passes):
                 k_pass = first + c
-                for b in range(2):
-                    nc.tensor.matmul_mx(
-                        out=p_sum[h][b][:],
-                        lhsT=rgb_codes[:, k_pass, :].bitcast(FP8X4),
-                        lhsT_scale=rgb_scales[:, k_pass, :],
-                        rhs=proj_codes[:, c, b * HALF : (b + 1) * HALF].bitcast(FP8X4),
-                        rhs_scale=proj_scales[:, c, b * HALF : (b + 1) * HALF],
-                        start=(k_pass == 0),
-                        stop=(k_pass == PASSES - 1),
-                    )
-
-        def finish_steps(h):
-            squares = tail.tile([T, HALF], BF16, name="squares")
-            half_sum = tail.tile([T, 2], F32, name="half_sum")
-            floored = tail.tile([T, 1], F32, name="floored")
-            inv_norm = tail.tile([T, 1], F32, name="inv_norm")
-            o_bf16 = tail.tile([T, PACK, P], BF16, name="o_bf16")
-            o_t = psum.tile([P, PACK, T], BF16, name="o_t")
-            o_grouped = tail.tile([P, T, PACK], BF16, name="o_grouped", align_bytes=64)
-            o_codes = tail.tile([P, T], U32, name="o_codes", align_bytes=64)
-            o_scales = tail.tile([P, T], U8, name="o_scales", align_bytes=64)
-            q_sum = []
-
-            def sum_squares():
-                for b in range(2):
-                    nc.scalar.activation(
-                        out=squares[:], in_=p_sum[h][b][:], func=ACT.Square, accum_out=half_sum[:, b : b + 1]
-                    )
-
-            def invert():
-                nc.vector.tensor_scalar(
-                    out=floored[:],
-                    in0=half_sum[:, 0:1],
-                    scalar1=half_sum[:, 1:2],
-                    scalar2=EPS * EPS,
-                    op0=ALU.add,
-                    op1=ALU.max,
-                )
-                nc.scalar.activation(out=inv_norm[:], in_=floored[:], func=ACT.Abs_reciprocal_sqrt)
-
-            def normalise():
-                nc.scalar.activation(
-                    out=o_bf16[:, :, : P // 2],
-                    in_=p_sum[h][0][:].rearrange("t (q j) -> t j q", j=PACK),
-                    func=ACT.Copy,
-                    scale=inv_norm[:],
-                )
-                nc.vector.tensor_scalar_mul(
-                    out=o_bf16[:, :, P // 2 :],
-                    in0=p_sum[h][1][:].rearrange("t (q j) -> t j q", j=PACK),
-                    scalar1=inv_norm[:],
-                )
-                nc.scalar.activation(out=o_f32[h][:, :HALF], in_=p_sum[h][0][:], func=ACT.Copy, scale=inv_norm[:])
-                nc.vector.tensor_scalar_mul(out=o_f32[h][:, HALF:], in0=p_sum[h][1][:], scalar1=inv_norm[:])
-
-            def transpose():
-                for j in range(PACK):
-                    nc.tensor.matmul(o_t[:, j, :], lhsT=o_bf16[:, j, :], rhs=identity[:], start=True, stop=True)
-
-            def regroup():
-                nc.scalar.copy(out=o_grouped[:], in_=o_t[:].rearrange("p j t -> p t j"))
-
-            def quantise_o():
-                nc.vector.quantize_mx(
-                    out=o_codes[:].bitcast(FP8X4),
-                    scales=o_scales[:],
-                    in_=o_grouped[:].rearrange("p t j -> p (t j)"),
+                nc.tensor.matmul_mx(
+                    out=p_sum[h][:],
+                    lhsT=rgb_codes[:, k_pass, :].bitcast(FP8X4),
+                    lhsT_scale=rgb_scales[:, k_pass, :],
+                    rhs=codes[:, c, :].bitcast(FP8X4),
+                    rhs_scale=scales[:, c, :],
+                    start=(k_pass == 0),
+                    stop=(k_pass == PASSES - 1),
                 )
 
-            def multiply():
-                for b in range(2):
-                    half = sums.tile([T, HALF], F32, name="q_half", tag="sum_%d" % b)
-                    nc.tensor.matmul_mx(
-                        out=half[:],
-                        lhsT=o_codes[:].bitcast(FP8X4),
-                        lhsT_scale=o_scales[:],
-                        rhs=atte_codes[:, h, b * HALF : (b + 1) * HALF].bitcast(FP8X4),
-                        rhs_scale=atte_scales[:, h, b * HALF : (b + 1) * HALF],
-                        start=True,
-                        stop=True,
-                    )
-                    q_sum.append(half)
 
-            def copy_q():
-                nc.scalar.copy(out=q_f32[h][:, :HALF], in_=q_sum[0][:])
-                nc.vector.tensor_copy(out=q_f32[h][:, HALF:], in_=q_sum[1][:])
+        def sum_squares(h):
+            nc.scalar.activation(out=squares[h][:], in_=p_sum[h][:], func=ACT.Square, accum_out=sum_sq[h][:])
 
-            return [sum_squares, invert, normalise, transpose, regroup, quantise_o, multiply, copy_q]
+        def floor(h):
+            nc.vector.tensor_scalar_max(out=floored[h][:], in0=sum_sq[h][:], scalar1=EPS * EPS)
+
+        def normalise(h):
+            nc.scalar.activation(out=inv_norm[h][:], in_=floored[h][:], func=ACT.Abs_reciprocal_sqrt)
+            nc.scalar.activation(
+                out=o_bf16[h][:],
+                in_=p_sum[h][:].rearrange("t (q j) -> t j q", j=PACK),
+                func=ACT.Copy,
+                scale=inv_norm[h][:],
+            )
+            nc.scalar.activation(out=o_f32[h][:], in_=p_sum[h][:], func=ACT.Copy, scale=inv_norm[h][:])
+
+        def transpose(h):
+            for j in range(PACK):
+                nc.tensor.matmul(o_t[h][:, j, :], lhsT=o_bf16[h][:, j, :], rhs=identity[:], start=True, stop=True)
+
+        def regroup_o(h):
+            nc.scalar.copy(out=o_grouped[h][:], in_=o_t[h][:].rearrange("p j t -> p t j"))
+
+        def quantise_o(h):
+            nc.vector.quantize_mx(
+                out=o_codes[h][:].bitcast(FP8X4),
+                scales=o_scales[h][:],
+                in_=o_grouped[h][:].rearrange("p t j -> p (t j)"),
+            )
+
+        def multiply_o(h, out, columns):
+            nc.tensor.matmul_mx(
+                out=out,
+                lhsT=o_codes[h][:].bitcast(FP8X4),
+                lhsT_scale=o_scales[h][:],
+                rhs=atte_codes[:, h, columns].bitcast(FP8X4),
+                rhs_scale=atte_scales[:, h, columns],
+                start=True,
+                stop=True,
+            )
 
         stream = []
         rgb_sizes = RGB_LOADS
         rgb_passes = 0
         for h in range(H):
             first = 0
-            for u, passes in enumerate(PROJ_LOADS[h]):
+            for passes in PROJ_LOADS[h]:
                 while rgb_passes < first + passes:
                     rows = rgb[0, rgb_passes * K_PASS : (rgb_passes + rgb_sizes[0]) * K_PASS, :]
                     rows = rows.rearrange("(c p j) t -> p c j t", p=P, j=PACK)
                     stream.append((finish_rgb, (rgb_passes, rgb_sizes[0]), rows, rgb_sizes[0], T, "rgb"))
                     rgb_passes += rgb_sizes[0]
                     rgb_sizes = rgb_sizes[1:]
-                if h == H - 1 and u == ATTE_SLOT:
-                    rows = atte_w.rearrange("h (p j) n -> p h j n", p=P, j=PACK)
-                    stream.append((finish_atte, (), rows, H, DH, "proj"))
                 rows = rgb_proj[h, first * K_PASS : (first + passes) * K_PASS, :]
                 rows = rows.rearrange("(c p j) f -> p c j f", p=P, j=PACK)
                 stream.append((finish_proj, (h, first, passes), rows, passes, DH, "proj"))
@@ -210,25 +178,51 @@ def tile_mca_pa_k_kernel(tc, rgb, rgb_proj, atte_w, out_0, out_1):
 
         steps = []
         waiting = None
-        for entry in stream + [None]:
-            grouped = None
-            if entry is not None:
-                grouped = load_and_regroup(nc, raw_pool, grouped_pool, entry[2], entry[3], entry[4], entry[5])
+        for complete, args, rows, passes, width, label in stream:
+            raw = raw_pool.tile([P, passes, PACK, width], BF16, name="raw_" + label, tag="raw_" + label)
+            nc.sync.dma_start(out=raw[:], in_=rows)
+            grouped = grouped_pool.tile(
+                [P, passes, width, PACK], BF16, name="grouped_" + label, tag="grouped_" + label, align_bytes=64
+            )
+            regroup(nc, raw[:], grouped[:])
             if steps:
-                steps[0]()
+                steps[0](0)
                 steps = steps[1:]
             if waiting is not None:
-                finish, args, tile_grouped = waiting
-                finish(*args, tile_grouped)
-                if finish is finish_proj and args[1] + args[2] == PASSES:
-                    steps = finish_steps(args[0])
-            if entry is not None:
-                waiting = (entry[0], entry[1], grouped)
-        for step in steps:
-            step()
+                waiting[0](*waiting[1], waiting[2])
+                if waiting[0] is finish_proj and waiting[1][1] + waiting[1][2] == PASSES:
+                    steps = [sum_squares, floor, normalise, transpose, regroup_o, quantise_o]
+            waiting = (complete, args, grouped)
+        waiting[0](*waiting[1], waiting[2])
+
+        atte_raw = []
+        for h in (1, 0):
+            raw = raw_pool.tile([P, 1, PACK, DH], BF16, name="raw_proj", tag="raw_proj")
+            nc.sync.dma_start(out=raw[:], in_=atte_w[h : h + 1, :, :].rearrange("c (p j) n -> p c j n", p=P, j=PACK))
+            atte_raw = [raw] + atte_raw
+        atte_grouped = [
+            grouped_pool.tile([P, 1, DH, PACK], BF16, name="grouped_proj", tag="grouped_proj", align_bytes=64)
+            for h in range(H)
+        ]
+        regroup(nc, atte_raw[1][:], atte_grouped[1][:])
+        finish_atte(1, atte_grouped[1])
+        sum_squares(1)
+        floor(1)
+        normalise(1)
+        transpose(1)
+        interleave(nc.vector.tensor_copy, atte_raw[0][:], atte_grouped[0][:])
+        finish_atte(0, atte_grouped[0])
+        multiply_o(0, q_sum_0[:], slice(0, DH))
+        regroup_o(1)
+        quantise_o(1)
+        nc.scalar.copy(out=q_f32[0][:], in_=q_sum_0[:])
+        for b in range(2):
+            multiply_o(1, q_halves_1[b][:], slice(b * HALF, (b + 1) * HALF))
+        nc.scalar.copy(out=q_f32[1][:, :HALF], in_=q_halves_1[0][:])
+        nc.vector.tensor_copy(out=q_f32[1][:, HALF:], in_=q_halves_1[1][:])
         nc.sync.dma_start(out=out_0[0, 0, :, :], in_=o_f32[0][:])
-        nc.sync.dma_start(out=out_1[0, 0, :, :], in_=q_f32[0][:])
         nc.sync.dma_start(out=out_0[0, 1, :, :], in_=o_f32[1][:])
+        nc.sync.dma_start(out=out_1[0, 0, :, :], in_=q_f32[0][:])
         for b in range(2):
             cols = slice(b * HALF, (b + 1) * HALF)
             nc.sync.dma_start(out=out_1[0, 1, :, cols], in_=q_f32[1][:, cols])

@@ -21,6 +21,8 @@ PASSES = D // K_PASS
 
 RGB_LOADS = [2, 2] + [4] * 7
 PROJ_LOADS = [[1, 1] + [2] * 15, [2] * 15 + [1, 1]]
+LONE_SCALAR_COLUMNS = 208
+WARM_UP = 3
 RUN = 8
 
 FLOPS = 2 * H * T * D * DH + 2 * H * T * DH * DH
@@ -34,15 +36,15 @@ def interleave(copy, raw, grouped):
 
 
 def regroup(nc, raw, grouped):
-    passes, width = raw.shape[1], raw.shape[3]
+    passes = raw.shape[1]
     if passes > 1:
         half = passes // 2
         interleave(nc.scalar.copy, raw[:, :half, :, :], grouped[:, :half, :, :])
         interleave(nc.vector.tensor_copy, raw[:, half:, :, :], grouped[:, half:, :, :])
     else:
-        half = width // 2
-        interleave(nc.scalar.copy, raw[:, :, :, :half], grouped[:, :, :half, :])
-        interleave(nc.vector.tensor_copy, raw[:, :, :, half:], grouped[:, :, half:, :])
+        split = LONE_SCALAR_COLUMNS
+        interleave(nc.scalar.copy, raw[:, :, :, :split], grouped[:, :, :split, :])
+        interleave(nc.vector.tensor_copy, raw[:, :, :, split:], grouped[:, :, split:, :])
 
 
 def tile_mca_pa_k_kernel(tc, rgb, rgb_proj, atte_w, out_0, out_1):
@@ -71,6 +73,7 @@ def tile_mca_pa_k_kernel(tc, rgb, rgb_proj, atte_w, out_0, out_1):
         p_sum = [sums.tile([T, DH], F32, name="p_sum%d" % h) for h in range(H)]
         o_f32 = [keep.tile([T, DH], F32, name="o_f32_%d" % h) for h in range(H)]
         q_f32 = [keep.tile([T, DH], F32, name="q_f32_%d" % h) for h in range(H)]
+        idle_sum = sums.tile([P, DH], F32, name="idle_sum")
         q_sum_0 = sums.tile([T, DH], F32, name="q_sum_0")
         q_halves_1 = [sums.tile([T, HALF], F32, name="q_half_%d" % b) for b in range(2)]
         squares = [keep.tile([T, DH], BF16, name="squares_%d" % h) for h in range(H)]
@@ -126,12 +129,14 @@ def tile_mca_pa_k_kernel(tc, rgb, rgb_proj, atte_w, out_0, out_1):
 
         def normalise(h):
             nc.scalar.activation(out=inv_norm[h][:], in_=floored[h][:], func=ACT.Abs_reciprocal_sqrt)
-            nc.scalar.activation(
-                out=o_bf16[h][:],
-                in_=p_sum[h][:].rearrange("t (q j) -> t j q", j=PACK),
-                func=ACT.Copy,
-                scale=inv_norm[h][:],
-            )
+            p_by_slot = p_sum[h][:].rearrange("t (q j) -> t j q", j=PACK)
+            for j in range(0, PACK, 2):
+                nc.scalar.activation(
+                    out=o_bf16[h][:, j : j + 2, :],
+                    in_=p_by_slot[:, j : j + 2, :],
+                    func=ACT.Copy,
+                    scale=inv_norm[h][:],
+                )
             nc.scalar.activation(out=o_f32[h][:], in_=p_sum[h][:], func=ACT.Copy, scale=inv_norm[h][:])
 
         def transpose(h):
@@ -180,7 +185,11 @@ def tile_mca_pa_k_kernel(tc, rgb, rgb_proj, atte_w, out_0, out_1):
         waiting = None
         for complete, args, rows, passes, width, label in stream:
             raw = raw_pool.tile([P, passes, PACK, width], BF16, name="raw_" + label, tag="raw_" + label)
-            nc.sync.dma_start(out=raw[:], in_=rows)
+            if complete is finish_proj:
+                for c in range(passes):
+                    nc.sync.dma_start(out=raw[:, c, :, :], in_=rows[:, c, :, :])
+            else:
+                nc.sync.dma_start(out=raw[:], in_=rows)
             grouped = grouped_pool.tile(
                 [P, passes, width, PACK], BF16, name="grouped_" + label, tag="grouped_" + label, align_bytes=64
             )
@@ -194,6 +203,10 @@ def tile_mca_pa_k_kernel(tc, rgb, rgb_proj, atte_w, out_0, out_1):
                     steps = [sum_squares, floor, normalise, transpose, regroup_o, quantise_o]
             waiting = (complete, args, grouped)
         waiting[0](*waiting[1], waiting[2])
+        for i in range(WARM_UP):
+            nc.tensor.matmul(
+                idle_sum[:], lhsT=identity[:], rhs=o_bf16[0][:].rearrange("t j q -> t (j q)"), start=True, stop=True
+            )
 
         atte_raw = []
         for h in (1, 0):

@@ -22,7 +22,8 @@ PASSES = D // K_PASS
 RGB_LOADS = [2, 2] + [4] * 7
 PROJ_LOADS = [[1, 1] + [2] * 15, [2] * 15 + [1, 1]]
 LONE_SCALAR_COLUMNS = 208
-WARM_UP = 3
+MOVE_EVERY = 5
+MOVED_SCALAR_COLUMNS = 128
 RUN = 8
 
 FLOPS = 2 * H * T * D * DH + 2 * H * T * DH * DH
@@ -35,6 +36,11 @@ def interleave(copy, raw, grouped):
     )
 
 
+def regroup_columns(nc, raw, grouped, split):
+    interleave(nc.scalar.copy, raw[:, :, :, :split], grouped[:, :, :split, :])
+    interleave(nc.vector.tensor_copy, raw[:, :, :, split:], grouped[:, :, split:, :])
+
+
 def regroup(nc, raw, grouped):
     passes = raw.shape[1]
     if passes > 1:
@@ -42,9 +48,7 @@ def regroup(nc, raw, grouped):
         interleave(nc.scalar.copy, raw[:, :half, :, :], grouped[:, :half, :, :])
         interleave(nc.vector.tensor_copy, raw[:, half:, :, :], grouped[:, half:, :, :])
     else:
-        split = LONE_SCALAR_COLUMNS
-        interleave(nc.scalar.copy, raw[:, :, :, :split], grouped[:, :, :split, :])
-        interleave(nc.vector.tensor_copy, raw[:, :, :, split:], grouped[:, :, split:, :])
+        regroup_columns(nc, raw, grouped, LONE_SCALAR_COLUMNS)
 
 
 def tile_mca_pa_k_kernel(tc, rgb, rgb_proj, atte_w, out_0, out_1):
@@ -53,7 +57,9 @@ def tile_mca_pa_k_kernel(tc, rgb, rgb_proj, atte_w, out_0, out_1):
         keep = ctx.enter_context(tc.tile_pool(name="keep", bufs=1))
         raw_pool = ctx.enter_context(tc.tile_pool(name="raw", bufs=8))
         grouped_pool = ctx.enter_context(tc.tile_pool(name="grouped", bufs=3))
-        mx_pool = ctx.enter_context(tc.tile_pool(name="mx", bufs=3))
+        mx_pool = ctx.enter_context(tc.tile_pool(name="mx", bufs=4))
+        moved_pool = ctx.enter_context(tc.psum_pool(name="moved", bufs=1))
+        turn_pool = ctx.enter_context(tc.psum_pool(name="turn", bufs=1))
         sums = ctx.enter_context(tc.psum_pool(name="sums", bufs=1))
         ctx.enter_context(tc.manual_schedule())
 
@@ -73,7 +79,6 @@ def tile_mca_pa_k_kernel(tc, rgb, rgb_proj, atte_w, out_0, out_1):
         p_sum = [sums.tile([T, DH], F32, name="p_sum%d" % h) for h in range(H)]
         o_f32 = [keep.tile([T, DH], F32, name="o_f32_%d" % h) for h in range(H)]
         q_f32 = [keep.tile([T, DH], F32, name="q_f32_%d" % h) for h in range(H)]
-        idle_sum = sums.tile([P, DH], F32, name="idle_sum")
         q_sum_0 = sums.tile([T, DH], F32, name="q_sum_0")
         q_halves_1 = [sums.tile([T, HALF], F32, name="q_half_%d" % b) for b in range(2)]
         squares = [keep.tile([T, DH], BF16, name="squares_%d" % h) for h in range(H)]
@@ -81,7 +86,7 @@ def tile_mca_pa_k_kernel(tc, rgb, rgb_proj, atte_w, out_0, out_1):
         floored = [keep.tile([T, 1], F32, name="floored_%d" % h) for h in range(H)]
         inv_norm = [keep.tile([T, 1], F32, name="inv_norm_%d" % h) for h in range(H)]
         o_bf16 = [keep.tile([T, PACK, P], BF16, name="o_bf16_%d" % h) for h in range(H)]
-        o_t = [sums.tile([P, PACK, T], BF16, name="o_t_%d" % h) for h in range(H)]
+        o_t = [turn_pool.tile([P, PACK, T], BF16, name="o_t") for h in range(H)]
         o_grouped = [keep.tile([P, T, PACK], BF16, name="o_grouped_%d" % h, align_bytes=64) for h in range(H)]
         o_codes = [keep.tile([P, T], U32, name="o_codes_%d" % h, align_bytes=64) for h in range(H)]
         o_scales = [keep.tile([P, T], U8, name="o_scales_%d" % h, align_bytes=64) for h in range(H)]
@@ -119,6 +124,21 @@ def tile_mca_pa_k_kernel(tc, rgb, rgb_proj, atte_w, out_0, out_1):
                     start=(k_pass == 0),
                     stop=(k_pass == PASSES - 1),
                 )
+
+        def move(raw):
+            banks = []
+            for b in range(2):
+                bank = moved_pool.tile([P, HALF, PACK], BF16, name="moved_%d" % b)
+                for j in range(0, PACK, 2):
+                    nc.tensor.matmul(
+                        bank[:, :, j : j + 2].rearrange("p w j -> p j w"),
+                        lhsT=identity[:],
+                        rhs=raw[:, j : j + 2, b * HALF : (b + 1) * HALF],
+                        start=True,
+                        stop=True,
+                    )
+                banks.append(bank)
+            return banks
 
 
         def sum_squares(h):
@@ -165,11 +185,12 @@ def tile_mca_pa_k_kernel(tc, rgb, rgb_proj, atte_w, out_0, out_1):
             )
 
         stream = []
+        moved_tiles = set()
         rgb_sizes = RGB_LOADS
         rgb_passes = 0
         for h in range(H):
             first = 0
-            for passes in PROJ_LOADS[h]:
+            for u, passes in enumerate(PROJ_LOADS[h]):
                 while rgb_passes < first + passes:
                     rows = rgb[0, rgb_passes * K_PASS : (rgb_passes + rgb_sizes[0]) * K_PASS, :]
                     rows = rows.rearrange("(c p j) t -> p c j t", p=P, j=PACK)
@@ -178,22 +199,40 @@ def tile_mca_pa_k_kernel(tc, rgb, rgb_proj, atte_w, out_0, out_1):
                     rgb_sizes = rgb_sizes[1:]
                 rows = rgb_proj[h, first * K_PASS : (first + passes) * K_PASS, :]
                 rows = rows.rearrange("(c p j) f -> p c j f", p=P, j=PACK)
+                if u % MOVE_EVERY == MOVE_EVERY - 1:
+                    moved_tiles.add(len(stream))
                 stream.append((finish_proj, (h, first, passes), rows, passes, DH, "proj"))
                 first += passes
 
-        steps = []
-        waiting = None
-        for complete, args, rows, passes, width, label in stream:
+        raws = []
+
+        def load(complete, args, rows, passes, width, label):
             raw = raw_pool.tile([P, passes, PACK, width], BF16, name="raw_" + label, tag="raw_" + label)
             if complete is finish_proj:
                 for c in range(passes):
                     nc.sync.dma_start(out=raw[:, c, :, :], in_=rows[:, c, :, :])
             else:
                 nc.sync.dma_start(out=raw[:], in_=rows)
+            raws.append(raw)
+
+        load(*stream[0])
+        steps = []
+        waiting = None
+        banks = []
+        for i, (complete, args, rows, passes, width, label) in enumerate(stream):
+            if i + 1 < len(stream):
+                load(*stream[i + 1])
+            raw = raws[i]
             grouped = grouped_pool.tile(
                 [P, passes, width, PACK], BF16, name="grouped_" + label, tag="grouped_" + label, align_bytes=64
             )
-            regroup(nc, raw[:], grouped[:])
+            if banks:
+                regroup_columns(nc, raw[:, 1:2, :, :], grouped[:, 1:2, :, :], MOVED_SCALAR_COLUMNS)
+                for b in range(2):
+                    nc.scalar.copy(out=grouped[:, 0, b * HALF : (b + 1) * HALF, :], in_=banks[b][:])
+            else:
+                regroup(nc, raw[:], grouped[:])
+            next_banks = move(raws[i + 1][:, 0, :, :]) if i + 1 in moved_tiles else []
             if steps:
                 steps[0](0)
                 steps = steps[1:]
@@ -202,11 +241,8 @@ def tile_mca_pa_k_kernel(tc, rgb, rgb_proj, atte_w, out_0, out_1):
                 if waiting[0] is finish_proj and waiting[1][1] + waiting[1][2] == PASSES:
                     steps = [sum_squares, floor, normalise, transpose, regroup_o, quantise_o]
             waiting = (complete, args, grouped)
+            banks = next_banks
         waiting[0](*waiting[1], waiting[2])
-        for i in range(WARM_UP):
-            nc.tensor.matmul(
-                idle_sum[:], lhsT=identity[:], rhs=o_bf16[0][:].rearrange("t j q -> t (j q)"), start=True, stop=True
-            )
 
         atte_raw = []
         for h in (1, 0):

@@ -23,7 +23,7 @@ RGB_LOADS = [2, 2] + [4] * 7
 PROJ_LOADS = [[1, 1] + [2] * 15, [2] * 15 + [1, 1]]
 LONE_SCALAR_COLUMNS = 208
 MOVE_EVERY = 5
-MOVED_SCALAR_COLUMNS = 128
+MOVED_SCALAR_COLUMNS = 192
 RUN = 8
 
 FLOPS = 2 * H * T * D * DH + 2 * H * T * DH * DH

from contextlib import ExitStack

import concourse.mybir as mybir
from concourse.masks import make_identity

BF16 = mybir.dt.bfloat16
F32 = mybir.dt.float32
U32 = mybir.dt.uint32
U8 = mybir.dt.uint8
FP8X4 = mybir.dt.float8_e4m3fn_x4
ACT = mybir.ActivationFunctionType

P = 128
PACK = 4
K_PASS = P * PACK

D, T, H, DH = 16384, 128, 2, 512
HALF = DH // 2
EPS = 1e-12
PASSES = D // K_PASS

RGB_LOADS = [2, 2] + [4] * 7
PROJ_LOADS = [[1, 1] + [2] * 15, [2] * 15 + [1, 1]]
LONE_SCALAR_COLUMNS = 208
MOVE_EVERY = 5
MOVED_SCALAR_COLUMNS = 192
RUN = 8

FLOPS = 2 * H * T * D * DH + 2 * H * T * DH * DH


def interleave(copy, raw, grouped):
    copy(
        out=grouped.rearrange("p c (g i) j -> p c g j i", i=RUN),
        in_=raw.rearrange("p c j (g i) -> p c g j i", i=RUN),
    )


def regroup_columns(nc, raw, grouped, split):
    interleave(nc.scalar.copy, raw[:, :, :, :split], grouped[:, :, :split, :])
    interleave(nc.vector.tensor_copy, raw[:, :, :, split:], grouped[:, :, split:, :])


def regroup(nc, raw, grouped):
    passes = raw.shape[1]
    if passes > 1:
        half = passes // 2
        interleave(nc.scalar.copy, raw[:, :half, :, :], grouped[:, :half, :, :])
        interleave(nc.vector.tensor_copy, raw[:, half:, :, :], grouped[:, half:, :, :])
    else:
        regroup_columns(nc, raw, grouped, LONE_SCALAR_COLUMNS)


def tile_mca_pa_k_kernel(tc, rgb, rgb_proj, atte_w, out_0, out_1):
    nc = tc.nc
    with ExitStack() as ctx:
        keep = ctx.enter_context(tc.tile_pool(name="keep", bufs=1))
        raw_pool = ctx.enter_context(tc.tile_pool(name="raw", bufs=8))
        grouped_pool = ctx.enter_context(tc.tile_pool(name="grouped", bufs=3))
        mx_pool = ctx.enter_context(tc.tile_pool(name="mx", bufs=4))
        moved_pool = ctx.enter_context(tc.psum_pool(name="moved", bufs=1))
        turn_pool = ctx.enter_context(tc.psum_pool(name="turn", bufs=1))
        sums = ctx.enter_context(tc.psum_pool(name="sums", bufs=1))
        ctx.enter_context(tc.manual_schedule())

        one = keep.tile([P, 1], F32, name="one")
        nc.vector.memset(one[:], 1.0)
        warm = keep.tile([P, 1], F32, name="warm")
        nc.scalar.activation(out=warm[:], in_=one[:], func=ACT.Abs_reciprocal_sqrt)

        identity = keep.tile([P, P], BF16, name="identity")
        make_identity(nc, identity[:])

        rgb_codes = keep.tile([P, PASSES, T], U32, name="rgb_codes", align_bytes=64)
        rgb_scales = keep.tile([P, PASSES, T], U8, name="rgb_scales", align_bytes=64)
        atte_codes = keep.tile([P, H, DH], U32, name="atte_codes", align_bytes=64)
        atte_scales = keep.tile([P, H, DH], U8, name="atte_scales", align_bytes=64)

        p_sum = [sums.tile([T, DH], F32, name="p_sum%d" % h) for h in range(H)]
        o_f32 = [keep.tile([T, DH], F32, name="o_f32_%d" % h) for h in range(H)]
        q_f32 = [keep.tile([T, DH], F32, name="q_f32_%d" % h) for h in range(H)]
        q_sum_0 = sums.tile([T, DH], F32, name="q_sum_0")
        q_halves_1 = [sums.tile([T, HALF], F32, name="q_half_%d" % b) for b in range(2)]
        squares = [keep.tile([T, DH], BF16, name="squares_%d" % h) for h in range(H)]
        sum_sq = [keep.tile([T, 1], F32, name="sum_sq_%d" % h) for h in range(H)]
        floored = [keep.tile([T, 1], F32, name="floored_%d" % h) for h in range(H)]
        inv_norm = [keep.tile([T, 1], F32, name="inv_norm_%d" % h) for h in range(H)]
        o_bf16 = [keep.tile([T, PACK, P], BF16, name="o_bf16_%d" % h) for h in range(H)]
        o_t = [turn_pool.tile([P, PACK, T], BF16, name="o_t") for h in range(H)]
        o_grouped = [keep.tile([P, T, PACK], BF16, name="o_grouped_%d" % h, align_bytes=64) for h in range(H)]
        o_codes = [keep.tile([P, T], U32, name="o_codes_%d" % h, align_bytes=64) for h in range(H)]
        o_scales = [keep.tile([P, T], U8, name="o_scales_%d" % h, align_bytes=64) for h in range(H)]

        def finish_rgb(first, passes, grouped):
            nc.vector.quantize_mx(
                out=rgb_codes[:, first : first + passes, :].rearrange("p c t -> p (c t)").bitcast(FP8X4),
                scales=rgb_scales[:, first : first + passes, :].rearrange("p c t -> p (c t)"),
                in_=grouped[:].rearrange("p c t j -> p (c t j)"),
            )

        def finish_atte(h, grouped):
            nc.vector.quantize_mx(
                out=atte_codes[:, h, :].bitcast(FP8X4),
                scales=atte_scales[:, h, :],
                in_=grouped[:].rearrange("p c n j -> p (c n j)"),
            )

        def finish_proj(h, first, passes, grouped):
            codes = mx_pool.tile([P, passes, DH], U32, name="proj_codes", align_bytes=64)
            scales = mx_pool.tile([P, passes, DH], U8, name="proj_scales", align_bytes=64)
            nc.vector.quantize_mx(
                out=codes[:].rearrange("p c w -> p (c w)").bitcast(FP8X4),
                scales=scales[:].rearrange("p c w -> p (c w)"),
                in_=grouped[:].rearrange("p c w j -> p (c w j)"),
            )
            for c in range(passes):
                k_pass = first + c
                nc.tensor.matmul_mx(
                    out=p_sum[h][:],
                    lhsT=rgb_codes[:, k_pass, :].bitcast(FP8X4),
                    lhsT_scale=rgb_scales[:, k_pass, :],
                    rhs=codes[:, c, :].bitcast(FP8X4),
                    rhs_scale=scales[:, c, :],
                    start=(k_pass == 0),
                    stop=(k_pass == PASSES - 1),
                )

        def move(raw):
            banks = []
            for b in range(2):
                bank = moved_pool.tile([P, HALF, PACK], BF16, name="moved_%d" % b)
                for j in range(0, PACK, 2):
                    nc.tensor.matmul(
                        bank[:, :, j : j + 2].rearrange("p w j -> p j w"),
                        lhsT=identity[:],
                        rhs=raw[:, j : j + 2, b * HALF : (b + 1) * HALF],
                        start=True,
                        stop=True,
                    )
                banks.append(bank)
            return banks


        def sum_squares(h):
            nc.scalar.activation(out=squares[h][:], in_=p_sum[h][:], func=ACT.Square, accum_out=sum_sq[h][:])

        def floor(h):
            nc.vector.tensor_scalar_max(out=floored[h][:], in0=sum_sq[h][:], scalar1=EPS * EPS)

        def normalise(h):
            nc.scalar.activation(out=inv_norm[h][:], in_=floored[h][:], func=ACT.Abs_reciprocal_sqrt)
            p_by_slot = p_sum[h][:].rearrange("t (q j) -> t j q", j=PACK)
            for j in range(0, PACK, 2):
                nc.scalar.activation(
                    out=o_bf16[h][:, j : j + 2, :],
                    in_=p_by_slot[:, j : j + 2, :],
                    func=ACT.Copy,
                    scale=inv_norm[h][:],
                )
            nc.scalar.activation(out=o_f32[h][:], in_=p_sum[h][:], func=ACT.Copy, scale=inv_norm[h][:])

        def transpose(h):
            for j in range(PACK):
                nc.tensor.matmul(o_t[h][:, j, :], lhsT=o_bf16[h][:, j, :], rhs=identity[:], start=True, stop=True)

        def regroup_o(h):
            nc.scalar.copy(out=o_grouped[h][:], in_=o_t[h][:].rearrange("p j t -> p t j"))

        def quantise_o(h):
            nc.vector.quantize_mx(
                out=o_codes[h][:].bitcast(FP8X4),
                scales=o_scales[h][:],
                in_=o_grouped[h][:].rearrange("p t j -> p (t j)"),
            )

        def multiply_o(h, out, columns):
            nc.tensor.matmul_mx(
                out=out,
                lhsT=o_codes[h][:].bitcast(FP8X4),
                lhsT_scale=o_scales[h][:],
                rhs=atte_codes[:, h, columns].bitcast(FP8X4),
                rhs_scale=atte_scales[:, h, columns],
                start=True,
                stop=True,
            )

        stream = []
        moved_tiles = set()
        rgb_sizes = RGB_LOADS
        rgb_passes = 0
        for h in range(H):
            first = 0
            for u, passes in enumerate(PROJ_LOADS[h]):
                while rgb_passes < first + passes:
                    rows = rgb[0, rgb_passes * K_PASS : (rgb_passes + rgb_sizes[0]) * K_PASS, :]
                    rows = rows.rearrange("(c p j) t -> p c j t", p=P, j=PACK)
                    stream.append((finish_rgb, (rgb_passes, rgb_sizes[0]), rows, rgb_sizes[0], T, "rgb"))
                    rgb_passes += rgb_sizes[0]
                    rgb_sizes = rgb_sizes[1:]
                rows = rgb_proj[h, first * K_PASS : (first + passes) * K_PASS, :]
                rows = rows.rearrange("(c p j) f -> p c j f", p=P, j=PACK)
                if u % MOVE_EVERY == MOVE_EVERY - 1:
                    moved_tiles.add(len(stream))
                stream.append((finish_proj, (h, first, passes), rows, passes, DH, "proj"))
                first += passes

        raws = []

        def load(complete, args, rows, passes, width, label):
            raw = raw_pool.tile([P, passes, PACK, width], BF16, name="raw_" + label, tag="raw_" + label)
            if complete is finish_proj:
                for c in range(passes):
                    nc.sync.dma_start(out=raw[:, c, :, :], in_=rows[:, c, :, :])
            else:
                nc.sync.dma_start(out=raw[:], in_=rows)
            raws.append(raw)

        load(*stream[0])
        steps = []
        waiting = None
        banks = []
        for i, (complete, args, rows, passes, width, label) in enumerate(stream):
            if i + 1 < len(stream):
                load(*stream[i + 1])
            raw = raws[i]
            grouped = grouped_pool.tile(
                [P, passes, width, PACK], BF16, name="grouped_" + label, tag="grouped_" + label, align_bytes=64
            )
            if banks:
                regroup_columns(nc, raw[:, 1:2, :, :], grouped[:, 1:2, :, :], MOVED_SCALAR_COLUMNS)
                for b in range(2):
                    nc.scalar.copy(out=grouped[:, 0, b * HALF : (b + 1) * HALF, :], in_=banks[b][:])
            else:
                regroup(nc, raw[:], grouped[:])
            next_banks = move(raws[i + 1][:, 0, :, :]) if i + 1 in moved_tiles else []
            if steps:
                steps[0](0)
                steps = steps[1:]
            if waiting is not None:
                waiting[0](*waiting[1], waiting[2])
                if waiting[0] is finish_proj and waiting[1][1] + waiting[1][2] == PASSES:
                    steps = [sum_squares, floor, normalise, transpose, regroup_o, quantise_o]
            waiting = (complete, args, grouped)
            banks = next_banks
        waiting[0](*waiting[1], waiting[2])

        atte_raw = []
        for h in (1, 0):
            raw = raw_pool.tile([P, 1, PACK, DH], BF16, name="raw_proj", tag="raw_proj")
            nc.sync.dma_start(out=raw[:], in_=atte_w[h : h + 1, :, :].rearrange("c (p j) n -> p c j n", p=P, j=PACK))
            atte_raw = [raw] + atte_raw
        atte_grouped = [
            grouped_pool.tile([P, 1, DH, PACK], BF16, name="grouped_proj", tag="grouped_proj", align_bytes=64)
            for h in range(H)
        ]
        regroup(nc, atte_raw[1][:], atte_grouped[1][:])
        finish_atte(1, atte_grouped[1])
        sum_squares(1)
        floor(1)
        normalise(1)
        transpose(1)
        interleave(nc.vector.tensor_copy, atte_raw[0][:], atte_grouped[0][:])
        finish_atte(0, atte_grouped[0])
        multiply_o(0, q_sum_0[:], slice(0, DH))
        regroup_o(1)
        quantise_o(1)
        nc.scalar.copy(out=q_f32[0][:], in_=q_sum_0[:])
        for b in range(2):
            multiply_o(1, q_halves_1[b][:], slice(b * HALF, (b + 1) * HALF))
        nc.scalar.copy(out=q_f32[1][:, :HALF], in_=q_halves_1[0][:])
        nc.vector.tensor_copy(out=q_f32[1][:, HALF:], in_=q_halves_1[1][:])
        nc.sync.dma_start(out=out_0[0, 0, :, :], in_=o_f32[0][:])
        nc.sync.dma_start(out=out_0[0, 1, :, :], in_=o_f32[1][:])
        nc.sync.dma_start(out=out_1[0, 0, :, :], in_=q_f32[0][:])
        for b in range(2):
            cols = slice(b * HALF, (b + 1) * HALF)
            nc.sync.dma_start(out=out_1[0, 1, :, cols], in_=q_f32[1][:, cols])
